import numpy as np
import ml_dtypes


def mxq(x, axis, fmt="e4m3"):
    dtype, down = {"e4m3": (ml_dtypes.float8_e4m3fn, 7), "e5m2": (ml_dtypes.float8_e5m2, 14)}[fmt]
    v = np.moveaxis(np.asarray(x, np.float32).astype(ml_dtypes.bfloat16).astype(np.float64), axis, -1)
    blocks = v.reshape(v.shape[:-1] + (-1, 32))
    amax = np.abs(blocks).max(-1, keepdims=True)
    byte = np.maximum(np.where(amax > 0, np.frexp(amax)[1] - 1 + 127, 0) - down, 1)
    scale = np.exp2(byte - 127.0)
    codes = (blocks / scale).astype(np.float32).astype(dtype).astype(np.float64)
    return np.moveaxis((codes * scale).reshape(v.shape), -1, axis)


WIDE = False


def mx_kscale(k):
    if not WIDE:
        return np.ones(k)
    levels = np.array([10, -10, 5, -5, 0])
    a = np.random.permutation(np.resize(levels, k // 512 * 4)).reshape(k // 512, 4)
    idx = np.arange(k)
    return np.exp2(a[idx // 512, idx % 128 // 32])


BF16 = ml_dtypes.bfloat16


def bf(x):
    return np.asarray(x, np.float32).astype(BF16)


def f64(x):
    return np.asarray(x).astype(np.float64)


B, T, D, H = 1, 384, 2048, 16
HD = D // H
ROPE_BASE = 10000.0


def rope_table():
    theta = 1.0 / (ROPE_BASE ** (np.arange(0, HD, 2) / HD))
    angles = np.arange(T)[:, None] * theta[None, :]
    return np.stack([np.cos(angles), np.sin(angles)], axis=-1)


def apply_rotary_emb(v, f_tab):
    vr = v.reshape(*v.shape[:-1], -1, 2)
    f = f_tab[None, :, None, :, :]
    v0, v1 = vr[..., 0], vr[..., 1]
    f0, f1 = f[..., 0], f[..., 1]
    y = np.stack([v0 * f0 - v1 * f1, v0 * f1 + v1 * f0], axis=-1)
    return y.reshape(v.shape)


def setup_inputs():
    s = mx_kscale(D)
    return {"x": bf(np.random.standard_normal((B, T, D)) * s),
            "freqs_cis": bf(rope_table()),
            "wq": bf(np.random.standard_normal((D, D)) * 1.5 / np.sqrt(D) / s[None, :]),
            "wk": bf(np.random.standard_normal((D, D)) * 1.5 / np.sqrt(D) / s[None, :]),
            "wv": bf(np.random.standard_normal((D, D)) * 1.0 / np.sqrt(D) / s[None, :])}


def reference(x, freqs_cis, wq, wk, wv):
    xm = mxq(f64(x), 2, "e4m3")
    q = (xm @ mxq(f64(wq), 1, "e4m3").T).reshape(B, T, H, HD)
    k = (xm @ mxq(f64(wk), 1, "e4m3").T).reshape(B, T, H, HD)
    v = (xm @ mxq(f64(wv), 1, "e4m3").T).reshape(B, T, H, HD)
    f_tab = f64(freqs_cis)
    return apply_rotary_emb(q, f_tab), apply_rotary_emb(k, f_tab), v

@@ -1,0 +1,240 @@
+from contextlib import ExitStack
+
+import concourse.bass as bass
+import concourse.mybir as mybir
+import concourse.tile as tile
+from concourse.masks import make_identity
+
+FLOPS = 2 * 384 * 2048 * 6144
+
+F32 = mybir.dt.float32
+BF16 = mybir.dt.bfloat16
+U32 = mybir.dt.uint32
+U8 = mybir.dt.uint8
+FP8X4 = mybir.dt.float8_e4m3fn_x4
+MULT = mybir.AluOpType.mult
+ADD = mybir.AluOpType.add
+
+P = 128
+T_TILES = 3
+PASSES = 4
+UNIT = 256
+N_UNITS = 24
+W_BUFS = 10
+PIN = True
+
+
+def tile_attention_pa_kernel(tc, x, freqs_cis, wq, wk, wv, out_0, out_1, out_2):
+    nc = tc.nc
+    x2 = x.rearrange("b t k -> (b t) k")
+    oq = out_0.rearrange("b t h d -> (b t) (h d)")
+    ok = out_1.rearrange("b t h d -> (b t) (h d)")
+    ov = out_2.rearrange("b t h d -> (b t) (h d)")
+
+    units = []
+    for r in range(4):
+        for i in (2 * r, 2 * r + 1):
+            units.append((wq, i))
+            units.append((wk, i))
+        units.append((wv, 2 * r))
+        units.append((wv, 2 * r + 1))
+
+    with ExitStack() as ctx:
+        const = ctx.enter_context(tc.tile_pool(name="const", bufs=1))
+        wpool = ctx.enter_context(tc.tile_pool(name="wpool", bufs=W_BUFS))
+        xpool = ctx.enter_context(tc.tile_pool(name="xpool", bufs=3))
+        gpool = ctx.enter_context(tc.tile_pool(name="gpool", bufs=3))
+        cpool = ctx.enter_context(tc.tile_pool(name="cpool", bufs=3))
+        zpool = ctx.enter_context(tc.tile_pool(name="zpool", bufs=6))
+        ypool = ctx.enter_context(tc.tile_pool(name="ypool", bufs=6))
+        tps = ctx.enter_context(tc.psum_pool(name="tps", bufs=4))
+        ops = ctx.enter_context(tc.psum_pool(name="ops", bufs=4))
+        if PIN:
+            ctx.enter_context(tc.manual_schedule())
+
+        ident = const.tile([P, P], F32, name="ident")
+        make_identity(nc, ident[:])
+
+        ftab = const.tile([P, T_TILES, 128], BF16, name="ftab")
+        nc.scalar.dma_start(out=ftab[:], in_=freqs_cis.rearrange("(a p) j e -> p a (j e)", p=P))
+
+        xraw = []
+        for tt in range(T_TILES):
+            xr = xpool.tile([P, 2048], BF16, name="xr", tag="xr")
+            nc.sync.dma_start(out=xr[:], in_=x2[tt * P:(tt + 1) * P, :])
+            xraw.append(xr)
+
+        wtiles = {}
+
+        def load(n):
+            w, i = units[n]
+            wt = wpool.tile([P, 4096], BF16, name="wt", tag="wt")
+            nc.sync.dma_start(
+                out=wt[:].rearrange("p (r k) -> p r k", r=2),
+                in_=w[i * UNIT:(i + 1) * UNIT, :].rearrange("(p r) k -> p r k", r=2),
+            )
+            wtiles[n] = wt
+
+        for n in range(W_BUFS):
+            load(n)
+
+        tab = const.tile([P, T_TILES, 512], F32, name="tab")
+        tabv = tab[:].rearrange("p a (e b h j) -> p a e b h j", e=2, b=2, h=2)
+        fv = ftab[:].rearrange("p a (j e) -> p a j e", e=2)
+        for e, b, comp, sign in ((0, 0, 0, 1.0), (0, 1, 1, -1.0), (1, 0, 1, 1.0), (1, 1, 0, 1.0)):
+            src = fv[:, :, :, comp].unsqueeze(2).to_broadcast([P, T_TILES, 2, 64])
+            if sign > 0:
+                nc.vector.tensor_copy(out=tabv[:, :, e, b, :, :], in_=src)
+            else:
+                nc.vector.tensor_scalar_mul(out=tabv[:, :, e, b, :, :], in0=src, scalar1=-1.0)
+
+        xc = const.tile([P, T_TILES * 512], U32, name="xc", align_bytes=64)
+        xs = const.tile([P, T_TILES * 512], U8, name="xs", align_bytes=64)
+        for tt in range(T_TILES):
+            x32 = xraw[tt][:].bitcast(F32)
+            xg = xpool.tile([P, 2048], BF16, name="xg", tag="xg", align_bytes=64)
+            xg32 = xg[:].bitcast(F32)
+            for gp in range(2):
+                tb = tps.tile([P, 512], F32, name="tb", tag="tb")
+                for uu in range(2):
+                    for gg in range(2):
+                        c0 = (2 * gp + gg) * 256 + uu * 128
+                        nc.tensor.transpose(tb[:, uu * 256 + gg * 128:uu * 256 + gg * 128 + 128],
+                                            x32[:, c0:c0 + 128], ident[:])
+                nc.scalar.copy(
+                    out=xg32[:, gp * 512:(gp + 1) * 512].rearrange("p (g t u) -> p g t u", g=2, u=2),
+                    in_=tb[:].rearrange("p (u g t) -> p g t u", u=2, g=2),
+                )
+            nc.vector.quantize_mx(
+                out=xc[:, tt * 512:(tt + 1) * 512].bitcast(FP8X4),
+                scales=xs[:, tt * 512:(tt + 1) * 512],
+                in_=xg[:],
+            )
+
+        groups = {}
+        quant = {}
+
+        def transposes(n):
+            w32 = wtiles[n][:].bitcast(F32)
+            grp = gpool.tile([P, 4096], BF16, name="grp", tag="grp", align_bytes=64)
+            g32 = grp[:].bitcast(F32)
+            for g in range(PASSES):
+                tb = tps.tile([P, 512], F32, name="tb", tag="tb")
+                for uu in range(2):
+                    for r in range(2):
+                        c0 = r * 1024 + g * 256 + uu * 128
+                        nc.tensor.transpose(tb[:, uu * 256 + r * 128:uu * 256 + r * 128 + 128],
+                                            w32[:, c0:c0 + 128], ident[:])
+                nc.scalar.copy(
+                    out=g32[:, g * 512:(g + 1) * 512].rearrange("p (n u) -> p n u", u=2),
+                    in_=tb[:].rearrange("p (u n) -> p n u", u=2),
+                )
+            groups[n] = grp
+
+        def quantise(n):
+            codes = cpool.tile([P, 1024], U32, name="codes", tag="codes", align_bytes=64)
+            scl = cpool.tile([P, 1024], U8, name="scl", tag="scl", align_bytes=64)
+            nc.vector.quantize_mx(out=codes[:].bitcast(FP8X4), scales=scl[:], in_=groups[n][:])
+            quant[n] = (codes, scl)
+
+        acc = {}
+
+        def passes(n):
+            pair, f = n // 2, n % 2
+            codes, scl = quant[n]
+            for tt in range(T_TILES):
+                if f == 0:
+                    acc[(pair, tt)] = ops.tile([P, 512], F32, name="acc", tag="acc")
+                o = acc[(pair, tt)]
+                for g in range(PASSES):
+                    a0 = tt * 512 + g * 128
+                    nc.tensor.matmul_mx(
+                        out=o[:, f * 256:(f + 1) * 256],
+                        lhsT=xc[:, a0:a0 + 128].bitcast(FP8X4),
+                        lhsT_scale=xs[:, a0:a0 + 128],
+                        rhs=codes[:, g * 256:(g + 1) * 256].bitcast(FP8X4),
+                        rhs_scale=scl[:, g * 256:(g + 1) * 256],
+                        start=(g == 0),
+                        stop=(g == PASSES - 1),
+                    )
+
+        ztiles = {}
+        ytiles = {}
+
+        def products(pair, tt):
+            z = zpool.tile([P, 1024], F32, name="z", tag="z")
+            nc.vector.tensor_tensor(
+                out=z[:].rearrange("p (f e c) -> p f e c", f=2, e=2),
+                in0=acc[(pair, tt)][:].rearrange("p (f c) -> p f c", f=2).unsqueeze(2).to_broadcast([P, 2, 2, 256]),
+                in1=tab[:, tt, :].rearrange("p (e c) -> p e c", e=2).unsqueeze(1).to_broadcast([P, 2, 2, 256]),
+                op=MULT,
+            )
+            ztiles[(pair, tt)] = z
+
+        def sums(pair, tt):
+            r, i = pair // 3, pair % 3
+            if i == 0:
+                ytiles[(r, tt)] = ypool.tile([P, 2, 512], F32, name="yqk", tag="yqk")
+            y = ytiles[(r, tt)]
+            zv = ztiles[(pair, tt)][:].rearrange("p (f e b c) -> p f e b c", f=2, e=2, b=2)
+            nc.vector.tensor_tensor(
+                out=y[:, :, i * 256:(i + 1) * 256].rearrange("p f (c e) -> p f c e", e=2),
+                in0=zv[:, :, :, 0, :].rearrange("p f e c -> p f c e"),
+                in1=zv[:, :, :, 1, :].rearrange("p f e c -> p f c e"),
+                op=ADD,
+            )
+            if i == 1:
+                rows = slice(tt * P, (tt + 1) * P)
+                cols = slice(r * 512, (r + 1) * 512)
+                nc.sync.dma_start(out=oq[rows, cols], in_=y[:, 0, :])
+                nc.sync.dma_start(out=ok[rows, cols], in_=y[:, 1, :])
+
+        def vcopy(pair, tt):
+            r = pair // 3
+            yv = ypool.tile([P, 512], F32, name="yv", tag="yv")
+            dst = yv[:].rearrange("p (f c e) -> p f c e", f=2, e=2)
+            src = acc[(pair, tt)][:].rearrange("p (f e c) -> p f c e", f=2, e=2)
+            if r == 3 and tt == 1:
+                nc.vector.tensor_copy(out=dst, in_=src)
+            else:
+                nc.scalar.copy(out=dst, in_=src)
+            nc.sync.dma_start(out=ov[tt * P:(tt + 1) * P, r * 512:(r + 1) * 512], in_=yv[:])
+
+        transposes(0)
+        load(W_BUFS)
+        quantise(0)
+        for n in range(N_UNITS):
+            if n + 1 < N_UNITS:
+                transposes(n + 1)
+                if n + 1 + W_BUFS < N_UNITS:
+                    load(n + 1 + W_BUFS)
+            passes(n)
+            if n + 1 < N_UNITS:
+                quantise(n + 1)
+            r, s = n // 6, n % 6
+            p0, p1, p2 = 3 * r, 3 * r + 1, 3 * r + 2
+            if s == 1:
+                products(p0, 0)
+                products(p0, 1)
+            elif s == 2:
+                products(p0, 2)
+                sums(p0, 0)
+            elif s == 3:
+                products(p1, 0)
+                products(p1, 1)
+            elif s == 4:
+                products(p1, 2)
+                sums(p0, 1)
+                if r == 3:
+                    sums(p0, 2)
+            elif s == 5:
+                if r < 3:
+                    sums(p0, 2)
+                sums(p1, 0)
+                sums(p1, 1)
+                if r == 3:
+                    sums(p1, 2)
+                for tt in range(T_TILES):
+                    vcopy(p2, tt)
+            if s == 0 and r > 0:
+                sums(3 * (r - 1) + 1, 2)

@@ -20,7 +20,9 @@ T_TILES = 3
 PASSES = 4
 UNIT = 256
 N_UNITS = 24
-W_BUFS = 10
+W_BUFS = 8
+LAG = 2
+PAIRS = "qqqvqqqvqqvv"
 PIN = True
 
 
@@ -32,12 +34,16 @@ def tile_attention_pa_kernel(tc, x, freqs_cis, wq, wk, wv, out_0, out_1, out_2):
     ov = out_2.rearrange("b t h d -> (b t) (h d)")
 
     units = []
-    for r in range(4):
-        for i in (2 * r, 2 * r + 1):
+    index = []
+    for kind in PAIRS:
+        i = len([1 for k in PAIRS[:len(index)] if k == kind])
+        index.append(i)
+        if kind == "q":
             units.append((wq, i))
             units.append((wk, i))
-        units.append((wv, 2 * r))
-        units.append((wv, 2 * r + 1))
+        else:
+            units.append((wv, 2 * i))
+            units.append((wv, 2 * i + 1))
 
     with ExitStack() as ctx:
         const = ctx.enter_context(tc.tile_pool(name="const", bufs=1))
@@ -45,8 +51,9 @@ def tile_attention_pa_kernel(tc, x, freqs_cis, wq, wk, wv, out_0, out_1, out_2):
         xpool = ctx.enter_context(tc.tile_pool(name="xpool", bufs=3))
         gpool = ctx.enter_context(tc.tile_pool(name="gpool", bufs=3))
         cpool = ctx.enter_context(tc.tile_pool(name="cpool", bufs=3))
-        zpool = ctx.enter_context(tc.tile_pool(name="zpool", bufs=6))
+        zpool = ctx.enter_context(tc.tile_pool(name="zpool", bufs=8))
         ypool = ctx.enter_context(tc.tile_pool(name="ypool", bufs=6))
+        qkpool = ctx.enter_context(tc.tile_pool(name="qkpool", bufs=9))
         tps = ctx.enter_context(tc.psum_pool(name="tps", bufs=4))
         ops = ctx.enter_context(tc.psum_pool(name="ops", bufs=4))
         if PIN:
@@ -172,9 +179,9 @@ def tile_attention_pa_kernel(tc, x, freqs_cis, wq, wk, wv, out_0, out_1, out_2):
             ztiles[(pair, tt)] = z
 
         def sums(pair, tt):
-            r, i = pair // 3, pair % 3
+            r, i = index[pair] // 2, index[pair] % 2
             if i == 0:
-                ytiles[(r, tt)] = ypool.tile([P, 2, 512], F32, name="yqk", tag="yqk")
+                ytiles[(r, tt)] = qkpool.tile([P, 2, 512], F32, name="yqk", tag="yqk")
             y = ytiles[(r, tt)]
             zv = ztiles[(pair, tt)][:].rearrange("p (f e b c) -> p f e b c", f=2, e=2, b=2)
             nc.vector.tensor_tensor(
@@ -189,52 +196,45 @@ def tile_attention_pa_kernel(tc, x, freqs_cis, wq, wk, wv, out_0, out_1, out_2):
                 nc.sync.dma_start(out=oq[rows, cols], in_=y[:, 0, :])
                 nc.sync.dma_start(out=ok[rows, cols], in_=y[:, 1, :])
 
-        def vcopy(pair, tt):
-            r = pair // 3
+        def vcopy(pair, tt, on_vector):
+            r = index[pair]
             yv = ypool.tile([P, 512], F32, name="yv", tag="yv")
             dst = yv[:].rearrange("p (f c e) -> p f c e", f=2, e=2)
             src = acc[(pair, tt)][:].rearrange("p (f e c) -> p f c e", f=2, e=2)
-            if r == 3 and tt == 1:
+            if on_vector:
                 nc.vector.tensor_copy(out=dst, in_=src)
             else:
                 nc.scalar.copy(out=dst, in_=src)
             nc.sync.dma_start(out=ov[tt * P:(tt + 1) * P, r * 512:(r + 1) * 512], in_=yv[:])
 
-        transposes(0)
-        load(W_BUFS)
-        quantise(0)
+        for n in range(LAG):
+            transposes(n)
+            load(n + W_BUFS)
+            quantise(n)
+        waiting = []
         for n in range(N_UNITS):
-            if n + 1 < N_UNITS:
-                transposes(n + 1)
-                if n + 1 + W_BUFS < N_UNITS:
-                    load(n + 1 + W_BUFS)
+            ahead = n + LAG
+            if ahead < N_UNITS:
+                transposes(ahead)
+                if ahead + W_BUFS < N_UNITS:
+                    load(ahead + W_BUFS)
             passes(n)
-            if n + 1 < N_UNITS:
-                quantise(n + 1)
-            r, s = n // 6, n % 6
-            p0, p1, p2 = 3 * r, 3 * r + 1, 3 * r + 2
-            if s == 1:
-                products(p0, 0)
-                products(p0, 1)
-            elif s == 2:
-                products(p0, 2)
-                sums(p0, 0)
-            elif s == 3:
-                products(p1, 0)
-                products(p1, 1)
-            elif s == 4:
-                products(p1, 2)
-                sums(p0, 1)
-                if r == 3:
-                    sums(p0, 2)
-            elif s == 5:
-                if r < 3:
-                    sums(p0, 2)
-                sums(p1, 0)
-                sums(p1, 1)
-                if r == 3:
-                    sums(p1, 2)
+            pair, second = n // 2, n % 2
+            kind = PAIRS[pair]
+            if second and kind == "q":
+                products(pair, 0)
+                products(pair, 1)
+                waiting.extend([(pair, 0), (pair, 1)])
+            if not second and pair > 0 and PAIRS[pair - 1] == "q":
+                products(pair - 1, 2)
+                waiting.append((pair - 1, 2))
+            if second and kind == "v":
                 for tt in range(T_TILES):
-                    vcopy(p2, tt)
-            if s == 0 and r > 0:
-                sums(3 * (r - 1) + 1, 2)
+                    vcopy(pair, tt, n == N_UNITS - 1 and tt == 1)
+            take = 3 if kind == "v" else (0 if second else 1)
+            for item in waiting[:take]:
+                sums(item[0], item[1])
+            waiting = waiting[take:]
+            if ahead < N_UNITS:
+                quantise(ahead)
+        assert not waiting

@@ -23,7 +23,7 @@ N_UNITS = 24
 W_BUFS = 8
 LAG = 2
 PAIRS = "qqqvqqqvqqvv"
-PIN = True
+PIN = False
 
 
 def tile_attention_pa_kernel(tc, x, freqs_cis, wq, wk, wv, out_0, out_1, out_2):

@@ -23,7 +23,7 @@ N_UNITS = 24
 W_BUFS = 8
 LAG = 2
 PAIRS = "qqqvqqqvqqvv"
-PIN = False
+PIN = True
 
 
 def tile_attention_pa_kernel(tc, x, freqs_cis, wq, wk, wv, out_0, out_1, out_2):
@@ -132,10 +132,12 @@ def tile_attention_pa_kernel(tc, x, freqs_cis, wq, wk, wv, out_0, out_1, out_2):
                         c0 = r * 1024 + g * 256 + uu * 128
                         nc.tensor.transpose(tb[:, uu * 256 + r * 128:uu * 256 + r * 128 + 128],
                                             w32[:, c0:c0 + 128], ident[:])
-                nc.scalar.copy(
-                    out=g32[:, g * 512:(g + 1) * 512].rearrange("p (n u) -> p n u", u=2),
-                    in_=tb[:].rearrange("p (u n) -> p n u", u=2),
-                )
+                dst = g32[:, g * 512:(g + 1) * 512].rearrange("p (n u) -> p n u", u=2)
+                src = tb[:].rearrange("p (u n) -> p n u", u=2)
+                if g == PASSES - 1:
+                    nc.vector.tensor_copy(out=dst, in_=src)
+                else:
+                    nc.scalar.copy(out=dst, in_=src)
             groups[n] = grp
 
         def quantise(n):
@@ -184,7 +186,7 @@ def tile_attention_pa_kernel(tc, x, freqs_cis, wq, wk, wv, out_0, out_1, out_2):
                 ytiles[(r, tt)] = qkpool.tile([P, 2, 512], F32, name="yqk", tag="yqk")
             y = ytiles[(r, tt)]
             zv = ztiles[(pair, tt)][:].rearrange("p (f e b c) -> p f e b c", f=2, e=2, b=2)
-            nc.vector.tensor_tensor(
+            nc.gpsimd.tensor_tensor(
                 out=y[:, :, i * 256:(i + 1) * 256].rearrange("p f (c e) -> p f c e", e=2),
                 in0=zv[:, :, :, 0, :].rearrange("p f e c -> p f c e"),
                 in1=zv[:, :, :, 1, :].rearrange("p f e c -> p f c e"),
@@ -231,7 +233,7 @@ def tile_attention_pa_kernel(tc, x, freqs_cis, wq, wk, wv, out_0, out_1, out_2):
             if second and kind == "v":
                 for tt in range(T_TILES):
                     vcopy(pair, tt, n == N_UNITS - 1 and tt == 1)
-            take = 3 if kind == "v" else (0 if second else 1)
+            take = 3
             for item in waiting[:take]:
                 sums(item[0], item[1])
             waiting = waiting[take:]

@@ -132,12 +132,10 @@ def tile_attention_pa_kernel(tc, x, freqs_cis, wq, wk, wv, out_0, out_1, out_2):
                         c0 = r * 1024 + g * 256 + uu * 128
                         nc.tensor.transpose(tb[:, uu * 256 + r * 128:uu * 256 + r * 128 + 128],
                                             w32[:, c0:c0 + 128], ident[:])
-                dst = g32[:, g * 512:(g + 1) * 512].rearrange("p (n u) -> p n u", u=2)
-                src = tb[:].rearrange("p (u n) -> p n u", u=2)
-                if g == PASSES - 1:
-                    nc.vector.tensor_copy(out=dst, in_=src)
-                else:
-                    nc.scalar.copy(out=dst, in_=src)
+                nc.scalar.copy(
+                    out=g32[:, g * 512:(g + 1) * 512].rearrange("p (n u) -> p n u", u=2),
+                    in_=tb[:].rearrange("p (u n) -> p n u", u=2),
+                )
             groups[n] = grp
 
         def quantise(n):

@@ -95,8 +95,9 @@ def tile_attention_pa_kernel(tc, x, freqs_cis, wq, wk, wv, out_0, out_1, out_2):
             else:
                 nc.vector.tensor_scalar_mul(out=tabv[:, :, e, b, :, :], in0=src, scalar1=-1.0)
 
-        xc = const.tile([P, T_TILES * 512], U32, name="xc", align_bytes=64)
-        xs = const.tile([P, T_TILES * 512], U8, name="xs", align_bytes=64)
+        xc_all = const.tile([P, 48 + T_TILES * 512], U32, name="xc", align_bytes=256)
+        xc = xc_all[:, 48:]
+        xs = const.tile([P, T_TILES * PASSES * 256], U8, name="xs", align_bytes=256)
         for tt in range(T_TILES):
             x32 = xraw[tt][:].bitcast(F32)
             xg = xpool.tile([P, 2048], BF16, name="xg", tag="xg", align_bytes=64)
@@ -112,11 +113,13 @@ def tile_attention_pa_kernel(tc, x, freqs_cis, wq, wk, wv, out_0, out_1, out_2):
                     out=xg32[:, gp * 512:(gp + 1) * 512].rearrange("p (g t u) -> p g t u", g=2, u=2),
                     in_=tb[:].rearrange("p (u g t) -> p g t u", u=2, g=2),
                 )
-            nc.vector.quantize_mx(
-                out=xc[:, tt * 512:(tt + 1) * 512].bitcast(FP8X4),
-                scales=xs[:, tt * 512:(tt + 1) * 512],
-                in_=xg[:],
-            )
+            for g in range(PASSES):
+                a0 = (tt * PASSES + g) * 128
+                nc.vector.quantize_mx(
+                    out=xc[:, a0:a0 + 128].bitcast(FP8X4),
+                    scales=xs[:, 2 * a0:2 * a0 + 128],
+                    in_=xg[:, g * 512:(g + 1) * 512],
+                )
 
         groups = {}
         quant = {}
@@ -139,8 +142,8 @@ def tile_attention_pa_kernel(tc, x, freqs_cis, wq, wk, wv, out_0, out_1, out_2):
             groups[n] = grp
 
         def quantise(n):
-            codes = cpool.tile([P, 1024], U32, name="codes", tag="codes", align_bytes=64)
-            scl = cpool.tile([P, 1024], U8, name="scl", tag="scl", align_bytes=64)
+            codes = cpool.tile([P, 1024], U32, name="codes", tag="codes", align_bytes=256)
+            scl = cpool.tile([P, 1024], U8, name="scl", tag="scl", align_bytes=256)
             nc.vector.quantize_mx(out=codes[:].bitcast(FP8X4), scales=scl[:], in_=groups[n][:])
             quant[n] = (codes, scl)
 
@@ -158,7 +161,7 @@ def tile_attention_pa_kernel(tc, x, freqs_cis, wq, wk, wv, out_0, out_1, out_2):
                     nc.tensor.matmul_mx(
                         out=o[:, f * 256:(f + 1) * 256],
                         lhsT=xc[:, a0:a0 + 128].bitcast(FP8X4),
-                        lhsT_scale=xs[:, a0:a0 + 128],
+                        lhsT_scale=xs[:, 2 * a0:2 * a0 + 128],
                         rhs=codes[:, g * 256:(g + 1) * 256].bitcast(FP8X4),
                         rhs_scale=scl[:, g * 256:(g + 1) * 256],
                         start=(g == 0),
@@ -184,7 +187,7 @@ def tile_attention_pa_kernel(tc, x, freqs_cis, wq, wk, wv, out_0, out_1, out_2):
                 ytiles[(r, tt)] = qkpool.tile([P, 2, 512], F32, name="yqk", tag="yqk")
             y = ytiles[(r, tt)]
             zv = ztiles[(pair, tt)][:].rearrange("p (f e b c) -> p f e b c", f=2, e=2, b=2)
-            nc.gpsimd.tensor_tensor(
+            nc.vector.tensor_tensor(
                 out=y[:, :, i * 256:(i + 1) * 256].rearrange("p f (c e) -> p f c e", e=2),
                 in0=zv[:, :, :, 0, :].rearrange("p f e c -> p f c e"),
                 in1=zv[:, :, :, 1, :].rearrange("p f e c -> p f c e"),
@@ -231,7 +234,7 @@ def tile_attention_pa_kernel(tc, x, freqs_cis, wq, wk, wv, out_0, out_1, out_2):
             if second and kind == "v":
                 for tt in range(T_TILES):
                     vcopy(pair, tt, n == N_UNITS - 1 and tt == 1)
-            take = 3
+            take = 3 if kind == "v" else (0 if second else 1)
             for item in waiting[:take]:
                 sums(item[0], item[1])
             waiting = waiting[take:]

@@ -124,11 +124,13 @@ def tile_attention_pa_kernel(tc, x, freqs_cis, wq, wk, wv, out_0, out_1, out_2):
         groups = {}
         quant = {}
 
-        def transposes(n):
+        def transposes(n, half):
             w32 = wtiles[n][:].bitcast(F32)
-            grp = gpool.tile([P, 4096], BF16, name="grp", tag="grp", align_bytes=64)
+            if half == 0:
+                groups[n] = gpool.tile([P, 4096], BF16, name="grp", tag="grp", align_bytes=64)
+            grp = groups[n]
             g32 = grp[:].bitcast(F32)
-            for g in range(PASSES):
+            for g in range(2 * half, 2 * half + 2):
                 tb = tps.tile([P, 512], F32, name="tb", tag="tb")
                 for uu in range(2):
                     for r in range(2):
@@ -139,7 +141,6 @@ def tile_attention_pa_kernel(tc, x, freqs_cis, wq, wk, wv, out_0, out_1, out_2):
                     out=g32[:, g * 512:(g + 1) * 512].rearrange("p (n u) -> p n u", u=2),
                     in_=tb[:].rearrange("p (u n) -> p n u", u=2),
                 )
-            groups[n] = grp
 
         def quantise(n):
             codes = cpool.tile([P, 1024], U32, name="codes", tag="codes", align_bytes=256)
@@ -149,14 +150,14 @@ def tile_attention_pa_kernel(tc, x, freqs_cis, wq, wk, wv, out_0, out_1, out_2):
 
         acc = {}
 
-        def passes(n):
+        def passes(n, half):
             pair, f = n // 2, n % 2
             codes, scl = quant[n]
-            for tt in range(T_TILES):
-                if f == 0:
+            for tt, g in [(k // PASSES, k % PASSES) for k in range(6 * half, 6 * half + 6)]:
+                if f == 0 and g == 0:
                     acc[(pair, tt)] = ops.tile([P, 512], F32, name="acc", tag="acc")
                 o = acc[(pair, tt)]
-                for g in range(PASSES):
+                if True:
                     a0 = tt * 512 + g * 128
                     nc.tensor.matmul_mx(
                         out=o[:, f * 256:(f + 1) * 256],
@@ -211,17 +212,21 @@ def tile_attention_pa_kernel(tc, x, freqs_cis, wq, wk, wv, out_0, out_1, out_2):
             nc.sync.dma_start(out=ov[tt * P:(tt + 1) * P, r * 512:(r + 1) * 512], in_=yv[:])
 
         for n in range(LAG):
-            transposes(n)
+            transposes(n, 0)
+            transposes(n, 1)
             load(n + W_BUFS)
             quantise(n)
         waiting = []
         for n in range(N_UNITS):
             ahead = n + LAG
             if ahead < N_UNITS:
-                transposes(ahead)
+                transposes(ahead, 0)
+            passes(n, 0)
+            if ahead < N_UNITS:
+                transposes(ahead, 1)
                 if ahead + W_BUFS < N_UNITS:
                     load(ahead + W_BUFS)
-            passes(n)
+            passes(n, 1)
             pair, second = n // 2, n % 2
             kind = PAIRS[pair]
             if second and kind == "q":

@@ -24,6 +24,8 @@ W_BUFS = 8
 LAG = 2
 PAIRS = "qqqvqqqvqqvv"
 PIN = True
+FINE_FROM = 3
+RUN = 2
 
 
 def tile_attention_pa_kernel(tc, x, freqs_cis, wq, wk, wv, out_0, out_1, out_2):
@@ -124,23 +126,23 @@ def tile_attention_pa_kernel(tc, x, freqs_cis, wq, wk, wv, out_0, out_1, out_2):
         groups = {}
         quant = {}
 
-        def transposes(n, half):
+        def transposes(n, g):
             w32 = wtiles[n][:].bitcast(F32)
-            if half == 0:
+            if g == 0:
                 groups[n] = gpool.tile([P, 4096], BF16, name="grp", tag="grp", align_bytes=64)
-            grp = groups[n]
-            g32 = grp[:].bitcast(F32)
-            for g in range(2 * half, 2 * half + 2):
-                tb = tps.tile([P, 512], F32, name="tb", tag="tb")
-                for uu in range(2):
-                    for r in range(2):
-                        c0 = r * 1024 + g * 256 + uu * 128
-                        nc.tensor.transpose(tb[:, uu * 256 + r * 128:uu * 256 + r * 128 + 128],
-                                            w32[:, c0:c0 + 128], ident[:])
-                nc.scalar.copy(
-                    out=g32[:, g * 512:(g + 1) * 512].rearrange("p (n u) -> p n u", u=2),
-                    in_=tb[:].rearrange("p (u n) -> p n u", u=2),
-                )
+            g32 = groups[n][:].bitcast(F32)
+            tb = tps.tile([P, 512], F32, name="tb", tag="tb")
+            for uu in range(2):
+                for r in range(2):
+                    c0 = r * 1024 + g * 256 + uu * 128
+                    nc.tensor.transpose(tb[:, uu * 256 + r * 128:uu * 256 + r * 128 + 128],
+                                        w32[:, c0:c0 + 128], ident[:])
+            nc.scalar.copy(
+                out=g32[:, g * 512:(g + 1) * 512].rearrange("p (n u) -> p n u", u=2),
+                in_=tb[:].rearrange("p (u n) -> p n u", u=2),
+            )
+            if g == PASSES - 1 and n + W_BUFS < N_UNITS:
+                load(n + W_BUFS)
 
         def quantise(n):
             codes = cpool.tile([P, 1024], U32, name="codes", tag="codes", align_bytes=256)
@@ -150,24 +152,21 @@ def tile_attention_pa_kernel(tc, x, freqs_cis, wq, wk, wv, out_0, out_1, out_2):
 
         acc = {}
 
-        def passes(n, half):
+        def one_pass(n, tt, g):
             pair, f = n // 2, n % 2
             codes, scl = quant[n]
-            for tt, g in [(k // PASSES, k % PASSES) for k in range(6 * half, 6 * half + 6)]:
-                if f == 0 and g == 0:
-                    acc[(pair, tt)] = ops.tile([P, 512], F32, name="acc", tag="acc")
-                o = acc[(pair, tt)]
-                if True:
-                    a0 = tt * 512 + g * 128
-                    nc.tensor.matmul_mx(
-                        out=o[:, f * 256:(f + 1) * 256],
-                        lhsT=xc[:, a0:a0 + 128].bitcast(FP8X4),
-                        lhsT_scale=xs[:, 2 * a0:2 * a0 + 128],
-                        rhs=codes[:, g * 256:(g + 1) * 256].bitcast(FP8X4),
-                        rhs_scale=scl[:, g * 256:(g + 1) * 256],
-                        start=(g == 0),
-                        stop=(g == PASSES - 1),
-                    )
+            if f == 0 and g == 0:
+                acc[(pair, tt)] = ops.tile([P, 512], F32, name="acc", tag="acc")
+            a0 = tt * 512 + g * 128
+            nc.tensor.matmul_mx(
+                out=acc[(pair, tt)][:, f * 256:(f + 1) * 256],
+                lhsT=xc[:, a0:a0 + 128].bitcast(FP8X4),
+                lhsT_scale=xs[:, 2 * a0:2 * a0 + 128],
+                rhs=codes[:, g * 256:(g + 1) * 256].bitcast(FP8X4),
+                rhs_scale=scl[:, g * 256:(g + 1) * 256],
+                start=(g == 0),
+                stop=(g == PASSES - 1),
+            )
 
         ztiles = {}
         ytiles = {}
@@ -194,8 +193,12 @@ def tile_attention_pa_kernel(tc, x, freqs_cis, wq, wk, wv, out_0, out_1, out_2):
                 in1=zv[:, :, :, 1, :].rearrange("p f e c -> p f c e"),
                 op=ADD,
             )
-            if i == 1:
-                rows = slice(tt * P, (tt + 1) * P)
+            rows = slice(tt * P, (tt + 1) * P)
+            if r >= FINE_FROM:
+                cols = slice(r * 512 + i * 256, r * 512 + (i + 1) * 256)
+                nc.sync.dma_start(out=oq[rows, cols], in_=y[:, 0, i * 256:(i + 1) * 256])
+                nc.sync.dma_start(out=ok[rows, cols], in_=y[:, 1, i * 256:(i + 1) * 256])
+            elif i == 1:
                 cols = slice(r * 512, (r + 1) * 512)
                 nc.sync.dma_start(out=oq[rows, cols], in_=y[:, 0, :])
                 nc.sync.dma_start(out=ok[rows, cols], in_=y[:, 1, :])
@@ -212,37 +215,37 @@ def tile_attention_pa_kernel(tc, x, freqs_cis, wq, wk, wv, out_0, out_1, out_2):
             nc.sync.dma_start(out=ov[tt * P:(tt + 1) * P, r * 512:(r + 1) * 512], in_=yv[:])
 
         for n in range(LAG):
-            transposes(n, 0)
-            transposes(n, 1)
-            load(n + W_BUFS)
+            for g in range(PASSES):
+                transposes(n, g)
             quantise(n)
+        banks = [(n, g) for n in range(LAG, N_UNITS) for g in range(PASSES)]
+        todo = [(n, tt, g) for n in range(N_UNITS) for tt in range(T_TILES) for g in range(PASSES)]
         waiting = []
-        for n in range(N_UNITS):
-            ahead = n + LAG
-            if ahead < N_UNITS:
-                transposes(ahead, 0)
-            passes(n, 0)
-            if ahead < N_UNITS:
-                transposes(ahead, 1)
-                if ahead + W_BUFS < N_UNITS:
-                    load(ahead + W_BUFS)
-            passes(n, 1)
-            pair, second = n // 2, n % 2
-            kind = PAIRS[pair]
-            if second and kind == "q":
-                products(pair, 0)
-                products(pair, 1)
-                waiting.extend([(pair, 0), (pair, 1)])
-            if not second and pair > 0 and PAIRS[pair - 1] == "q":
-                products(pair - 1, 2)
-                waiting.append((pair - 1, 2))
-            if second and kind == "v":
-                for tt in range(T_TILES):
-                    vcopy(pair, tt, n == N_UNITS - 1 and tt == 1)
-            take = 3 if kind == "v" else (0 if second else 1)
-            for item in waiting[:take]:
-                sums(item[0], item[1])
-            waiting = waiting[take:]
-            if ahead < N_UNITS:
-                quantise(ahead)
+        for step in range((len(todo) + 3 * RUN - 1) // (3 * RUN)):
+            for n, g in banks[step * RUN:(step + 1) * RUN]:
+                transposes(n, g)
+            for n, tt, g in todo[step * 3 * RUN:(step + 1) * 3 * RUN]:
+                one_pass(n, tt, g)
+                if tt == T_TILES - 1 and g == PASSES - 1:
+                    ahead = n + LAG
+                    pair, second = n // 2, n % 2
+                    kind = PAIRS[pair]
+                    if second and kind == "q":
+                        products(pair, 0)
+                        products(pair, 1)
+                        waiting.extend([(pair, 0), (pair, 1)])
+                    if not second and pair > 0 and PAIRS[pair - 1] == "q":
+                        products(pair - 1, 2)
+                        waiting.append((pair - 1, 2))
+                    if second and kind == "v":
+                        for t3 in range(T_TILES):
+                            vcopy(pair, t3, n == N_UNITS - 1 and t3 == 1)
+                    if ahead < N_UNITS and kind == "v":
+                        quantise(ahead)
+                    take = 3 if kind == "v" else (0 if second else 1)
+                    for item in waiting[:take]:
+                        sums(item[0], item[1])
+                    waiting = waiting[take:]
+                    if ahead < N_UNITS and kind == "q":
+                        quantise(ahead)
         assert not waiting

from contextlib import ExitStack

import concourse.bass as bass
import concourse.mybir as mybir
import concourse.tile as tile
from concourse.masks import make_identity

FLOPS = 2 * 384 * 2048 * 6144

F32 = mybir.dt.float32
BF16 = mybir.dt.bfloat16
U32 = mybir.dt.uint32
U8 = mybir.dt.uint8
FP8X4 = mybir.dt.float8_e4m3fn_x4
MULT = mybir.AluOpType.mult
ADD = mybir.AluOpType.add

P = 128
T_TILES = 3
PASSES = 4
UNIT = 256
N_UNITS = 24
W_BUFS = 8
LAG = 2
PAIRS = "qqqvqqqvqqvv"
PIN = True
FINE_FROM = 3
RUN = 2


def tile_attention_pa_kernel(tc, x, freqs_cis, wq, wk, wv, out_0, out_1, out_2):
    nc = tc.nc
    x2 = x.rearrange("b t k -> (b t) k")
    oq = out_0.rearrange("b t h d -> (b t) (h d)")
    ok = out_1.rearrange("b t h d -> (b t) (h d)")
    ov = out_2.rearrange("b t h d -> (b t) (h d)")

    units = []
    index = []
    for kind in PAIRS:
        i = len([1 for k in PAIRS[:len(index)] if k == kind])
        index.append(i)
        if kind == "q":
            units.append((wq, i))
            units.append((wk, i))
        else:
            units.append((wv, 2 * i))
            units.append((wv, 2 * i + 1))

    with ExitStack() as ctx:
        const = ctx.enter_context(tc.tile_pool(name="const", bufs=1))
        wpool = ctx.enter_context(tc.tile_pool(name="wpool", bufs=W_BUFS))
        xpool = ctx.enter_context(tc.tile_pool(name="xpool", bufs=3))
        gpool = ctx.enter_context(tc.tile_pool(name="gpool", bufs=3))
        cpool = ctx.enter_context(tc.tile_pool(name="cpool", bufs=3))
        zpool = ctx.enter_context(tc.tile_pool(name="zpool", bufs=8))
        ypool = ctx.enter_context(tc.tile_pool(name="ypool", bufs=6))
        qkpool = ctx.enter_context(tc.tile_pool(name="qkpool", bufs=9))
        tps = ctx.enter_context(tc.psum_pool(name="tps", bufs=4))
        ops = ctx.enter_context(tc.psum_pool(name="ops", bufs=4))
        if PIN:
            ctx.enter_context(tc.manual_schedule())

        ident = const.tile([P, P], F32, name="ident")
        make_identity(nc, ident[:])

        ftab = const.tile([P, T_TILES, 128], BF16, name="ftab")
        nc.scalar.dma_start(out=ftab[:], in_=freqs_cis.rearrange("(a p) j e -> p a (j e)", p=P))

        xraw = []
        for tt in range(T_TILES):
            xr = xpool.tile([P, 2048], BF16, name="xr", tag="xr")
            nc.sync.dma_start(out=xr[:], in_=x2[tt * P:(tt + 1) * P, :])
            xraw.append(xr)

        wtiles = {}

        def load(n):
            w, i = units[n]
            wt = wpool.tile([P, 4096], BF16, name="wt", tag="wt")
            nc.sync.dma_start(
                out=wt[:].rearrange("p (r k) -> p r k", r=2),
                in_=w[i * UNIT:(i + 1) * UNIT, :].rearrange("(p r) k -> p r k", r=2),
            )
            wtiles[n] = wt

        for n in range(W_BUFS):
            load(n)

        tab = const.tile([P, T_TILES, 512], F32, name="tab")
        tabv = tab[:].rearrange("p a (e b h j) -> p a e b h j", e=2, b=2, h=2)
        fv = ftab[:].rearrange("p a (j e) -> p a j e", e=2)
        for e, b, comp, sign in ((0, 0, 0, 1.0), (0, 1, 1, -1.0), (1, 0, 1, 1.0), (1, 1, 0, 1.0)):
            src = fv[:, :, :, comp].unsqueeze(2).to_broadcast([P, T_TILES, 2, 64])
            if sign > 0:
                nc.vector.tensor_copy(out=tabv[:, :, e, b, :, :], in_=src)
            else:
                nc.vector.tensor_scalar_mul(out=tabv[:, :, e, b, :, :], in0=src, scalar1=-1.0)

        xc_all = const.tile([P, 48 + T_TILES * 512], U32, name="xc", align_bytes=256)
        xc = xc_all[:, 48:]
        xs = const.tile([P, T_TILES * PASSES * 256], U8, name="xs", align_bytes=256)
        for tt in range(T_TILES):
            x32 = xraw[tt][:].bitcast(F32)
            xg = xpool.tile([P, 2048], BF16, name="xg", tag="xg", align_bytes=64)
            xg32 = xg[:].bitcast(F32)
            for gp in range(2):
                tb = tps.tile([P, 512], F32, name="tb", tag="tb")
                for uu in range(2):
                    for gg in range(2):
                        c0 = (2 * gp + gg) * 256 + uu * 128
                        nc.tensor.transpose(tb[:, uu * 256 + gg * 128:uu * 256 + gg * 128 + 128],
                                            x32[:, c0:c0 + 128], ident[:])
                nc.scalar.copy(
                    out=xg32[:, gp * 512:(gp + 1) * 512].rearrange("p (g t u) -> p g t u", g=2, u=2),
                    in_=tb[:].rearrange("p (u g t) -> p g t u", u=2, g=2),
                )
            for g in range(PASSES):
                a0 = (tt * PASSES + g) * 128
                nc.vector.quantize_mx(
                    out=xc[:, a0:a0 + 128].bitcast(FP8X4),
                    scales=xs[:, 2 * a0:2 * a0 + 128],
                    in_=xg[:, g * 512:(g + 1) * 512],
                )

        groups = {}
        quant = {}

        def transposes(n, g):
            w32 = wtiles[n][:].bitcast(F32)
            if g == 0:
                groups[n] = gpool.tile([P, 4096], BF16, name="grp", tag="grp", align_bytes=64)
            g32 = groups[n][:].bitcast(F32)
            tb = tps.tile([P, 512], F32, name="tb", tag="tb")
            for uu in range(2):
                for r in range(2):
                    c0 = r * 1024 + g * 256 + uu * 128
                    nc.tensor.transpose(tb[:, uu * 256 + r * 128:uu * 256 + r * 128 + 128],
                                        w32[:, c0:c0 + 128], ident[:])
            nc.scalar.copy(
                out=g32[:, g * 512:(g + 1) * 512].rearrange("p (n u) -> p n u", u=2),
                in_=tb[:].rearrange("p (u n) -> p n u", u=2),
            )
            if g == PASSES - 1 and n + W_BUFS < N_UNITS:
                load(n + W_BUFS)

        def quantise(n):
            codes = cpool.tile([P, 1024], U32, name="codes", tag="codes", align_bytes=256)
            scl = cpool.tile([P, 1024], U8, name="scl", tag="scl", align_bytes=256)
            nc.vector.quantize_mx(out=codes[:].bitcast(FP8X4), scales=scl[:], in_=groups[n][:])
            quant[n] = (codes, scl)

        acc = {}

        def one_pass(n, tt, g):
            pair, f = n // 2, n % 2
            codes, scl = quant[n]
            if f == 0 and g == 0:
                acc[(pair, tt)] = ops.tile([P, 512], F32, name="acc", tag="acc")
            a0 = tt * 512 + g * 128
            nc.tensor.matmul_mx(
                out=acc[(pair, tt)][:, f * 256:(f + 1) * 256],
                lhsT=xc[:, a0:a0 + 128].bitcast(FP8X4),
                lhsT_scale=xs[:, 2 * a0:2 * a0 + 128],
                rhs=codes[:, g * 256:(g + 1) * 256].bitcast(FP8X4),
                rhs_scale=scl[:, g * 256:(g + 1) * 256],
                start=(g == 0),
                stop=(g == PASSES - 1),
            )

        ztiles = {}
        ytiles = {}

        def products(pair, tt):
            z = zpool.tile([P, 1024], F32, name="z", tag="z")
            nc.vector.tensor_tensor(
                out=z[:].rearrange("p (f e c) -> p f e c", f=2, e=2),
                in0=acc[(pair, tt)][:].rearrange("p (f c) -> p f c", f=2).unsqueeze(2).to_broadcast([P, 2, 2, 256]),
                in1=tab[:, tt, :].rearrange("p (e c) -> p e c", e=2).unsqueeze(1).to_broadcast([P, 2, 2, 256]),
                op=MULT,
            )
            ztiles[(pair, tt)] = z

        def sums(pair, tt):
            r, i = index[pair] // 2, index[pair] % 2
            if i == 0:
                ytiles[(r, tt)] = qkpool.tile([P, 2, 512], F32, name="yqk", tag="yqk")
            y = ytiles[(r, tt)]
            zv = ztiles[(pair, tt)][:].rearrange("p (f e b c) -> p f e b c", f=2, e=2, b=2)
            nc.vector.tensor_tensor(
                out=y[:, :, i * 256:(i + 1) * 256].rearrange("p f (c e) -> p f c e", e=2),
                in0=zv[:, :, :, 0, :].rearrange("p f e c -> p f c e"),
                in1=zv[:, :, :, 1, :].rearrange("p f e c -> p f c e"),
                op=ADD,
            )
            rows = slice(tt * P, (tt + 1) * P)
            if r >= FINE_FROM:
                cols = slice(r * 512 + i * 256, r * 512 + (i + 1) * 256)
                nc.sync.dma_start(out=oq[rows, cols], in_=y[:, 0, i * 256:(i + 1) * 256])
                nc.sync.dma_start(out=ok[rows, cols], in_=y[:, 1, i * 256:(i + 1) * 256])
            elif i == 1:
                cols = slice(r * 512, (r + 1) * 512)
                nc.sync.dma_start(out=oq[rows, cols], in_=y[:, 0, :])
                nc.sync.dma_start(out=ok[rows, cols], in_=y[:, 1, :])

        def vcopy(pair, tt, on_vector):
            r = index[pair]
            yv = ypool.tile([P, 512], F32, name="yv", tag="yv")
            dst = yv[:].rearrange("p (f c e) -> p f c e", f=2, e=2)
            src = acc[(pair, tt)][:].rearrange("p (f e c) -> p f c e", f=2, e=2)
            if on_vector:
                nc.vector.tensor_copy(out=dst, in_=src)
            else:
                nc.scalar.copy(out=dst, in_=src)
            nc.sync.dma_start(out=ov[tt * P:(tt + 1) * P, r * 512:(r + 1) * 512], in_=yv[:])

        for n in range(LAG):
            for g in range(PASSES):
                transposes(n, g)
            quantise(n)
        banks = [(n, g) for n in range(LAG, N_UNITS) for g in range(PASSES)]
        todo = [(n, tt, g) for n in range(N_UNITS) for tt in range(T_TILES) for g in range(PASSES)]
        waiting = []
        for step in range((len(todo) + 3 * RUN - 1) // (3 * RUN)):
            for n, g in banks[step * RUN:(step + 1) * RUN]:
                transposes(n, g)
            for n, tt, g in todo[step * 3 * RUN:(step + 1) * 3 * RUN]:
                one_pass(n, tt, g)
                if tt == T_TILES - 1 and g == PASSES - 1:
                    ahead = n + LAG
                    pair, second = n // 2, n % 2
                    kind = PAIRS[pair]
                    if second and kind == "q":
                        products(pair, 0)
                        products(pair, 1)
                        waiting.extend([(pair, 0), (pair, 1)])
                    if not second and pair > 0 and PAIRS[pair - 1] == "q":
                        products(pair - 1, 2)
                        waiting.append((pair - 1, 2))
                    if second and kind == "v":
                        for t3 in range(T_TILES):
                            vcopy(pair, t3, n == N_UNITS - 1 and t3 == 1)
                    if ahead < N_UNITS and kind == "v":
                        quantise(ahead)
                    take = 3 if kind == "v" else (0 if second else 1)
                    for item in waiting[:take]:
                        sums(item[0], item[1])
                    waiting = waiting[take:]
                    if ahead < N_UNITS and kind == "q":
                        quantise(ahead)
        assert not waiting
